import numpy as np
import ml_dtypes


def mxq(x, axis, fmt="e4m3"):
    dtype, down = {"e4m3": (ml_dtypes.float8_e4m3fn, 7), "e5m2": (ml_dtypes.float8_e5m2, 14)}[fmt]
    v = np.moveaxis(np.asarray(x, np.float32).astype(ml_dtypes.bfloat16).astype(np.float64), axis, -1)
    blocks = v.reshape(v.shape[:-1] + (-1, 32))
    amax = np.abs(blocks).max(-1, keepdims=True)
    byte = np.maximum(np.where(amax > 0, np.frexp(amax)[1] - 1 + 127, 0) - down, 1)
    scale = np.exp2(byte - 127.0)
    codes = (blocks / scale).astype(np.float32).astype(dtype).astype(np.float64)
    return np.moveaxis((codes * scale).reshape(v.shape), -1, axis)


WIDE = False


def mx_kscale(k):
    if not WIDE:
        return np.ones(k)
    levels = np.array([10, -10, 5, -5, 0])
    a = np.random.permutation(np.resize(levels, k // 512 * 4)).reshape(k // 512, 4)
    idx = np.arange(k)
    return np.exp2(a[idx // 512, idx % 128 // 32])


BF16 = ml_dtypes.bfloat16


def bf(x):
    return np.asarray(x, np.float32).astype(BF16)


def f64(x):
    return np.asarray(x).astype(np.float64)


N, CH = 10240, 512

REPARAM_OFFSET = 2.0 ** (-18)
PEDESTAL = REPARAM_OFFSET ** 2
BETA_MIN = 1e-6
BETA_BOUND = (BETA_MIN + PEDESTAL) ** 0.5
GAMMA_BOUND = REPARAM_OFFSET


def setup_inputs():
    u = np.exp2(np.round(np.log2(mx_kscale(CH)) / 2))
    amp = np.exp(0.6 * np.random.standard_normal((N, 1)))
    x = np.random.standard_normal((N, CH)) * amp * u
    beta = (0.7 + 0.7 * np.random.standard_normal(CH)) * u
    gamma = np.random.standard_normal((CH, CH)) * np.sqrt(2.0 / CH) * u[:, None] / u[None, :]
    return {"x": bf(x), "beta": bf(beta), "gamma": bf(gamma)}


def reference(x, beta, gamma):
    x = f64(x)
    b = np.maximum(f64(beta), BETA_BOUND) ** 2 - PEDESTAL
    g = np.maximum(f64(gamma), GAMMA_BOUND) ** 2 - PEDESTAL
    norm = np.sqrt((mxq(x * x, 1, "e4m3") @ mxq(g, 1, "e4m3").T) + b)
    return x / norm

@@ -1,0 +1,203 @@
+from contextlib import ExitStack
+
+import concourse.masks as masks
+import concourse.mybir as mybir
+
+F32 = mybir.dt.float32
+BF16 = mybir.dt.bfloat16
+U32 = mybir.dt.uint32
+U8 = mybir.dt.uint8
+FP8X4 = mybir.dt.float8_e4m3fn_x4
+ACT = mybir.ActivationFunctionType
+ALU = mybir.AluOpType
+
+P = 128
+N_ROWS = 10240
+CH = 512
+CHUNK = 512
+NCH = N_ROWS // CHUNK
+FLOPS = 2 * N_ROWS * CH * CH
+
+PEDESTAL = 2.0 ** -36
+BETA_BOUND = (1e-6 + PEDESTAL) ** 0.5
+
+LX = 3
+NM = 3
+NR = 3
+NSQ = 4
+NCD = 3
+NRT = 3
+NO = 4
+USE_G = True
+HEAD_S = 3
+
+
+def tile_gdn_t_kernel(tc, x, beta, gamma, out):
+    nc = tc.nc
+    with ExitStack() as ctx:
+        keep = ctx.enter_context(tc.tile_pool(name="keep", bufs=1))
+        psum = ctx.enter_context(tc.psum_pool(name="psum", bufs=1))
+        ctx.enter_context(tc.manual_schedule())
+
+        ident = keep.tile([P, P], F32, name="ident")
+        warm = keep.tile([P, 1], F32, name="warm")
+        warm2 = keep.tile([P, 1], F32, name="warm2")
+        gam = keep.tile([P, 4, CH], BF16, name="gam")
+        bet = keep.tile([4, P], BF16, name="bet")
+        bz = keep.tile([P, P], F32, name="bz")
+        b1 = keep.tile([P, 4], F32, name="b1")
+        b2 = keep.tile([P, 4], F32, name="b2")
+        b_sb = keep.tile([P, 4], F32, name="b_sb")
+        gw = [keep.tile([P, 1024], BF16, name="gw%d" % i) for i in range(2)]
+        g2 = [keep.tile([P, 1024], F32, name="g2%d" % i) for i in range(2)]
+        gq = keep.tile([P, 2048], BF16, name="gq", align_bytes=64)
+        g_cd = keep.tile([P, CH], U32, name="g_cd", align_bytes=64)
+        g_sc = keep.tile([P, CH], U8, name="g_sc", align_bytes=64)
+        xs = [keep.tile([P, 4, CH], BF16, name="x%d" % c) for c in range(NCH)]
+        sq = [keep.tile([P, 2048], BF16, name="sq%d" % i, align_bytes=64) for i in range(NSQ)]
+        tmp = [keep.tile([P, 1024], BF16, name="tmp%d" % i) for i in range(2)]
+        cd = [keep.tile([P, CHUNK], U32, name="cd%d" % i, align_bytes=64) for i in range(NCD)]
+        sc = [keep.tile([P, CHUNK], U8, name="sc%d" % i, align_bytes=64) for i in range(NCD)]
+        rt = [keep.tile([P, 4, CHUNK], F32, name="rt%d" % i) for i in range(NRT)]
+        ot = [keep.tile([P, 4, CH], F32, name="ot%d" % i) for i in range(NO)]
+
+        xb = [psum.tile([P, 512], F32, name="xb%d" % i) for i in range(2)]
+        mb = [psum.tile([P, 512], F32, name="mb%d" % i) for i in range(NM)]
+        rb = [psum.tile([P, 512], F32, name="rb%d" % i) for i in range(NR)]
+
+        xv = x.rearrange("(c p r) j -> c p r j", p=P, r=4)
+        ov = out.rearrange("(c p r) i -> c p r i", p=P, r=4)
+
+        nc.scalar.dma_start(out=bet[:], in_=beta.rearrange("(m p) -> m p", p=P))
+        nc.sync.dma_start(out=gam[:], in_=gamma.rearrange("(m p) j -> p m j", p=P))
+        for c in range(NCH):
+            nc.sync.dma_start(out=xs[c][:], in_=xv[c, :, :, :])
+        masks.make_identity(nc, ident[:])
+        nc.vector.memset(warm[:], 1.0)
+        nc.scalar.activation(out=warm2[:], in_=warm[:], func=ACT.Abs_reciprocal_sqrt)
+        nc.vector.memset(bz[:], 0.0)
+        nc.vector.tensor_copy(out=bz[0:4, :], in_=bet[:])
+        nc.tensor.transpose(rb[0][:, 0:P], bz[:], ident[:])
+        nc.vector.tensor_scalar_max(out=b1[:], in0=rb[0][:, 0:4], scalar1=BETA_BOUND)
+        nc.vector.tensor_tensor(out=b2[:], in0=b1[:], in1=b1[:], op=ALU.mult)
+        nc.vector.tensor_scalar_add(out=b_sb[:], in0=b2[:], scalar1=-PEDESTAL)
+
+        def words_to_bank(bank, src, half):
+            for u in range(2):
+                col = u * 256 + half * P
+                nc.tensor.transpose(bank[:, col:col + P], src.bitcast(F32)[:, u * P:(u + 1) * P], ident[:])
+
+        def bank_words(bank):
+            return bank[:].rearrange("p (u n) -> p n u", u=2)
+
+        def grouped_words(dst):
+            return dst.bitcast(F32).rearrange("p (n u) -> p n u", u=2)
+
+        for hb in range(2):
+            for mm in range(2):
+                words_to_bank(xb[hb], gam[:, 2 * hb + mm, :], mm)
+            nc.scalar.copy(out=grouped_words(gw[hb][:]), in_=bank_words(xb[hb]))
+
+        def g_chain(hb, step):
+            cols = slice(hb * 1024, (hb + 1) * 1024)
+            wcols = slice(hb * 256, (hb + 1) * 256)
+            if step == 0:
+                nc.vector.scalar_tensor_tensor(out=g2[hb][:], in0=gw[hb][:], scalar=0.0, in1=gw[hb][:],
+                                               op0=ALU.max, op1=ALU.mult)
+            elif step == 1:
+                nc.vector.tensor_scalar(out=gq[:, cols], in0=g2[hb][:], scalar1=PEDESTAL, scalar2=-PEDESTAL,
+                                        op0=ALU.max, op1=ALU.add)
+            else:
+                nc.vector.quantize_mx(out=g_cd[:, wcols].bitcast(FP8X4), scales=g_sc[:, wcols], in_=gq[:, cols])
+
+        def ok(c):
+            return 0 <= c < NCH
+
+        def xt(c, h):
+            if ok(c):
+                for rr in range(2):
+                    words_to_bank(xb[h], xs[c][:, 2 * h + rr, :], rr)
+
+        def sq_dst(c, h):
+            return sq[c % NSQ][:, h * 1024:(h + 1) * 1024]
+
+        def sq_scalar(c, h):
+            nc.scalar.activation(
+                out=sq_dst(c, h).rearrange("p (n u e) -> p n u e", u=2, e=2),
+                in_=xb[h][:].bitcast(BF16).rearrange("p (u n e) -> p n u e", u=2, e=2),
+                func=ACT.Square)
+
+        def sq_vector(c, h):
+            t = tmp[h]
+            nc.vector.tensor_copy(out=grouped_words(t[:]), in_=bank_words(xb[h]))
+            eng = nc.gpsimd if (USE_G and c >= HEAD_S) else nc.vector
+            eng.tensor_tensor(out=sq_dst(c, h), in0=t[:], in1=t[:], op=ALU.mult)
+
+        def quant(c):
+            if ok(c):
+                nc.vector.quantize_mx(out=cd[c % NCD][:].bitcast(FP8X4), scales=sc[c % NCD][:], in_=sq[c % NSQ][:])
+
+        def mx(c, m):
+            if ok(c):
+                cols = slice(m * P, (m + 1) * P)
+                nc.tensor.matmul_mx(out=mb[(4 * c + m) % NM][:],
+                                    lhsT=g_cd[:, cols].bitcast(FP8X4), lhsT_scale=g_sc[:, cols],
+                                    rhs=cd[c % NCD][:].bitcast(FP8X4), rhs_scale=sc[c % NCD][:],
+                                    start=True, stop=True)
+
+        def ars(c, m):
+            if ok(c):
+                nc.scalar.activation(out=rt[c % NRT][:, m, :], in_=mb[(4 * c + m) % NM][:],
+                                     func=ACT.Abs_reciprocal_sqrt, bias=b_sb[:, m:m + 1], scale=1.0)
+
+        def rtr(c, r):
+            if ok(c):
+                bank = rb[(4 * c + r) % NR]
+                for m in range(4):
+                    nc.tensor.transpose(bank[:, m * P:(m + 1) * P], rt[c % NRT][:, m, r * P:(r + 1) * P], ident[:])
+                nc.vector.tensor_tensor(out=ot[c % NO][:, r, :], in0=bank[:], in1=xs[c][:, r, :], op=ALU.mult)
+
+        def store(c):
+            if ok(c):
+                nc.sync.dma_start(out=ov[c, :, :, :], in_=ot[c % NO][:])
+
+        def on_scalar(c, h):
+            return h == 0 or c < HEAD_S
+
+        g_chain(0, 0)
+        g_chain(0, 1)
+        g_chain(0, 2)
+        deferred = []
+        for k in range(-LX, NCH + 2):
+            for m in range(2):
+                mx(k, m)
+            for m in range(2):
+                ars(k, m)
+            if k == -LX + 1:
+                g_chain(1, 0)
+            quant(k + 1)
+            if k == -LX + 1:
+                g_chain(1, 1)
+                g_chain(1, 2)
+            for (c, h) in deferred:
+                sq_vector(c, h)
+            deferred = []
+            rtr(k - 1, 0)
+            rtr(k - 1, 1)
+            for h in range(2):
+                c = k + LX
+                if h == 1:
+                    rtr(k - 1, 2)
+                xt(c, h)
+                if ok(c):
+                    if on_scalar(c, h):
+                        sq_scalar(c, h)
+                    else:
+                        deferred.append((c, h))
+                if h == 0:
+                    for m in range(2, 4):
+                        mx(k, m)
+                    for m in range(2, 4):
+                        ars(k, m)
+            rtr(k - 1, 3)
+            store(k - 1)

@@ -21,15 +21,21 @@ FLOPS = 2 * N_ROWS * CH * CH
 PEDESTAL = 2.0 ** -36
 BETA_BOUND = (1e-6 + PEDESTAL) ** 0.5
 
-LX = 3
+LX = 4
+QL = 2
 NM = 3
 NR = 3
-NSQ = 4
-NCD = 3
+NSQ = 6
+NCD = 4
 NRT = 3
 NO = 4
-USE_G = True
-HEAD_S = 3
+NTMP = 3
+
+
+def head_engine(c, h):
+    if c == 3 or (c == 2 and h == 0):
+        return "V"
+    return "S"
 
 
 def tile_gdn_t_kernel(tc, x, beta, gamma, out):
@@ -55,7 +61,7 @@ def tile_gdn_t_kernel(tc, x, beta, gamma, out):
         g_sc = keep.tile([P, CH], U8, name="g_sc", align_bytes=64)
         xs = [keep.tile([P, 4, CH], BF16, name="x%d" % c) for c in range(NCH)]
         sq = [keep.tile([P, 2048], BF16, name="sq%d" % i, align_bytes=64) for i in range(NSQ)]
-        tmp = [keep.tile([P, 1024], BF16, name="tmp%d" % i) for i in range(2)]
+        tmp = [keep.tile([P, 1024], BF16, name="tmp%d" % i) for i in range(NTMP)]
         cd = [keep.tile([P, CHUNK], U32, name="cd%d" % i, align_bytes=64) for i in range(NCD)]
         sc = [keep.tile([P, CHUNK], U8, name="sc%d" % i, align_bytes=64) for i in range(NCD)]
         rt = [keep.tile([P, 4, CHUNK], F32, name="rt%d" % i) for i in range(NRT)]
@@ -67,11 +73,16 @@ def tile_gdn_t_kernel(tc, x, beta, gamma, out):
 
         xv = x.rearrange("(c p r) j -> c p r j", p=P, r=4)
         ov = out.rearrange("(c p r) i -> c p r i", p=P, r=4)
+        gv = gamma.rearrange("(m p) j -> p m j", p=P)
 
         nc.scalar.dma_start(out=bet[:], in_=beta.rearrange("(m p) -> m p", p=P))
-        nc.sync.dma_start(out=gam[:], in_=gamma.rearrange("(m p) j -> p m j", p=P))
-        for c in range(NCH):
+        nc.sync.dma_start(out=gam[:, 0:2, :], in_=gv[:, 0:2, :])
+        nc.sync.dma_start(out=xs[0][:, 0:2, :], in_=xv[0, :, 0:2, :])
+        nc.sync.dma_start(out=gam[:, 2:4, :], in_=gv[:, 2:4, :])
+        nc.sync.dma_start(out=xs[0][:, 2:4, :], in_=xv[0, :, 2:4, :])
+        for c in range(1, NCH):
             nc.sync.dma_start(out=xs[c][:], in_=xv[c, :, :, :])
+
         masks.make_identity(nc, ident[:])
         nc.vector.memset(warm[:], 1.0)
         nc.scalar.activation(out=warm2[:], in_=warm[:], func=ACT.Abs_reciprocal_sqrt)
@@ -93,10 +104,10 @@ def tile_gdn_t_kernel(tc, x, beta, gamma, out):
         def grouped_words(dst):
             return dst.bitcast(F32).rearrange("p (n u) -> p n u", u=2)
 
-        for hb in range(2):
+        def g_turn(hb):
             for mm in range(2):
-                words_to_bank(xb[hb], gam[:, 2 * hb + mm, :], mm)
-            nc.scalar.copy(out=grouped_words(gw[hb][:]), in_=bank_words(xb[hb]))
+                words_to_bank(mb[hb], gam[:, 2 * hb + mm, :], mm)
+            nc.scalar.copy(out=grouped_words(gw[hb][:]), in_=bank_words(mb[hb]))
 
         def g_chain(hb, step):
             cols = slice(hb * 1024, (hb + 1) * 1024)
@@ -127,10 +138,11 @@ def tile_gdn_t_kernel(tc, x, beta, gamma, out):
                 in_=xb[h][:].bitcast(BF16).rearrange("p (u n e) -> p n u e", u=2, e=2),
                 func=ACT.Square)
 
-        def sq_vector(c, h):
-            t = tmp[h]
-            nc.vector.tensor_copy(out=grouped_words(t[:]), in_=bank_words(xb[h]))
-            eng = nc.gpsimd if (USE_G and c >= HEAD_S) else nc.vector
+        def sq_words(c, h):
+            nc.vector.tensor_copy(out=grouped_words(tmp[(2 * c + h) % NTMP][:]), in_=bank_words(xb[h]))
+
+        def sq_mul(c, h, eng):
+            t = tmp[(2 * c + h) % NTMP]
             eng.tensor_tensor(out=sq_dst(c, h), in0=t[:], in1=t[:], op=ALU.mult)
 
         def quant(c):
@@ -155,49 +167,71 @@ def tile_gdn_t_kernel(tc, x, beta, gamma, out):
                 bank = rb[(4 * c + r) % NR]
                 for m in range(4):
                     nc.tensor.transpose(bank[:, m * P:(m + 1) * P], rt[c % NRT][:, m, r * P:(r + 1) * P], ident[:])
-                nc.vector.tensor_tensor(out=ot[c % NO][:, r, :], in0=bank[:], in1=xs[c][:, r, :], op=ALU.mult)
 
-        def store(c):
+        def mul(c, r):
             if ok(c):
-                nc.sync.dma_start(out=ov[c, :, :, :], in_=ot[c % NO][:])
+                nc.vector.tensor_tensor(out=ot[c % NO][:, r, :], in0=rb[(4 * c + r) % NR][:], in1=xs[c][:, r, :],
+                                        op=ALU.mult)
 
-        def on_scalar(c, h):
-            return h == 0 or c < HEAD_S
+        def store(c, r0, r1):
+            if ok(c):
+                nc.sync.dma_start(out=ov[c, :, r0:r1, :], in_=ot[c % NO][:, r0:r1, :])
 
+        g_turn(0)
         g_chain(0, 0)
         g_chain(0, 1)
         g_chain(0, 2)
-        deferred = []
-        for k in range(-LX, NCH + 2):
-            for m in range(2):
-                mx(k, m)
-            for m in range(2):
-                ars(k, m)
+        pending = []
+        for k in range(-LX, NCH + 1):
+            c = k + LX
+            last = (k - 1 == NCH - 1)
+            mx(k, 0)
+            mx(k, 1)
+            xt(c, 0)
+            rtr(k - 1, 0)
+            rtr(k - 1, 1)
+            for (pc, ph) in pending:
+                sq_scalar(pc, ph)
+            pending = []
+            ars(k, 0)
+            ars(k, 1)
+            mul(k - 1, 0)
+            mul(k - 1, 1)
+            if last:
+                store(k - 1, 0, 2)
             if k == -LX + 1:
                 g_chain(1, 0)
-            quant(k + 1)
+            e0 = "G" if c >= LX else head_engine(c, 0)
+            if ok(c) and e0 == "S":
+                sq_scalar(c, 0)
+            if ok(c) and e0 != "S":
+                sq_words(c, 0)
+            if ok(c) and e0 == "V":
+                sq_mul(c, 0, nc.vector)
+            quant(k + QL)
+            if ok(c) and e0 == "G":
+                sq_mul(c, 0, nc.gpsimd)
+            if k == -LX:
+                g_turn(1)
             if k == -LX + 1:
                 g_chain(1, 1)
                 g_chain(1, 2)
-            for (c, h) in deferred:
-                sq_vector(c, h)
-            deferred = []
-            rtr(k - 1, 0)
-            rtr(k - 1, 1)
-            for h in range(2):
-                c = k + LX
-                if h == 1:
-                    rtr(k - 1, 2)
-                xt(c, h)
-                if ok(c):
-                    if on_scalar(c, h):
-                        sq_scalar(c, h)
-                    else:
-                        deferred.append((c, h))
-                if h == 0:
-                    for m in range(2, 4):
-                        mx(k, m)
-                    for m in range(2, 4):
-                        ars(k, m)
+            mx(k, 2)
+            mx(k, 3)
+            xt(c, 1)
+            rtr(k - 1, 2)
             rtr(k - 1, 3)
-            store(k - 1)
+            ars(k, 2)
+            ars(k, 3)
+            mul(k - 1, 2)
+            mul(k - 1, 3)
+            if last:
+                store(k - 1, 2, 4)
+            else:
+                store(k - 1, 0, 4)
+            e1 = "S" if c >= LX else head_engine(c, 1)
+            if ok(c) and e1 == "S":
+                pending.append((c, 1))
+            if ok(c) and e1 == "V":
+                sq_words(c, 1)
+                sq_mul(c, 1, nc.vector)

@@ -21,7 +21,7 @@ FLOPS = 2 * N_ROWS * CH * CH
 PEDESTAL = 2.0 ** -36
 BETA_BOUND = (1e-6 + PEDESTAL) ** 0.5
 
-LX = 4
+PL = 3
 QL = 2
 NM = 3
 NR = 3
@@ -32,8 +32,11 @@ NO = 4
 NTMP = 3
 
 
+HEAD = 4
+
+
 def head_engine(c, h):
-    if c == 3 or (c == 2 and h == 0):
+    if h == 1 and c != 1:
         return "V"
     return "S"
 
@@ -177,14 +180,20 @@ def tile_gdn_t_kernel(tc, x, beta, gamma, out):
             if ok(c):
                 nc.sync.dma_start(out=ov[c, :, r0:r1, :], in_=ot[c % NO][:, r0:r1, :])
 
+        def mul_store(c, r):
+            mul(c, r)
+            if c == NCH - 1:
+                store(c, r, r + 1)
+            elif r % 2 == 1:
+                store(c, r - 1, r + 1)
+
         g_turn(0)
         g_chain(0, 0)
         g_chain(0, 1)
         g_chain(0, 2)
         pending = []
-        for k in range(-LX, NCH + 1):
-            c = k + LX
-            last = (k - 1 == NCH - 1)
+        for k in range(-PL, NCH + 1):
+            c = k + 3 if k <= 0 else k + 4
             mx(k, 0)
             mx(k, 1)
             xt(c, 0)
@@ -195,13 +204,11 @@ def tile_gdn_t_kernel(tc, x, beta, gamma, out):
             pending = []
             ars(k, 0)
             ars(k, 1)
-            mul(k - 1, 0)
-            mul(k - 1, 1)
-            if last:
-                store(k - 1, 0, 2)
-            if k == -LX + 1:
+            mul_store(k - 1, 0)
+            mul_store(k - 1, 1)
+            if k == -PL + 1:
                 g_chain(1, 0)
-            e0 = "G" if c >= LX else head_engine(c, 0)
+            e0 = "G" if c >= HEAD else head_engine(c, 0)
             if ok(c) and e0 == "S":
                 sq_scalar(c, 0)
             if ok(c) and e0 != "S":
@@ -211,9 +218,9 @@ def tile_gdn_t_kernel(tc, x, beta, gamma, out):
             quant(k + QL)
             if ok(c) and e0 == "G":
                 sq_mul(c, 0, nc.gpsimd)
-            if k == -LX:
+            if k == -PL:
                 g_turn(1)
-            if k == -LX + 1:
+            if k == -PL + 1:
                 g_chain(1, 1)
                 g_chain(1, 2)
             mx(k, 2)
@@ -223,15 +230,17 @@ def tile_gdn_t_kernel(tc, x, beta, gamma, out):
             rtr(k - 1, 3)
             ars(k, 2)
             ars(k, 3)
-            mul(k - 1, 2)
-            mul(k - 1, 3)
-            if last:
-                store(k - 1, 2, 4)
-            else:
-                store(k - 1, 0, 4)
-            e1 = "S" if c >= LX else head_engine(c, 1)
+            mul_store(k - 1, 2)
+            mul_store(k - 1, 3)
+            e1 = "S" if c >= HEAD else head_engine(c, 1)
             if ok(c) and e1 == "S":
                 pending.append((c, 1))
             if ok(c) and e1 == "V":
                 sq_words(c, 1)
                 sq_mul(c, 1, nc.vector)
+            if k == 0:
+                xt(4, 0)
+                sq_words(4, 0)
+                sq_mul(4, 0, nc.gpsimd)
+                xt(4, 1)
+                pending.append((4, 1))

@@ -196,13 +196,13 @@ def tile_gdn_t_kernel(tc, x, beta, gamma, out):
             c = k + 3 if k <= 0 else k + 4
             mx(k, 0)
             mx(k, 1)
-            xt(c, 0)
             rtr(k - 1, 0)
+            xt(c, 0)
             rtr(k - 1, 1)
+            ars(k, 0)
             for (pc, ph) in pending:
                 sq_scalar(pc, ph)
             pending = []
-            ars(k, 0)
             ars(k, 1)
             mul_store(k - 1, 0)
             mul_store(k - 1, 1)
@@ -225,8 +225,8 @@ def tile_gdn_t_kernel(tc, x, beta, gamma, out):
                 g_chain(1, 2)
             mx(k, 2)
             mx(k, 3)
-            xt(c, 1)
             rtr(k - 1, 2)
+            xt(c, 1)
             rtr(k - 1, 3)
             ars(k, 2)
             ars(k, 3)

@@ -46,7 +46,6 @@ def tile_gdn_t_kernel(tc, x, beta, gamma, out):
     with ExitStack() as ctx:
         keep = ctx.enter_context(tc.tile_pool(name="keep", bufs=1))
         psum = ctx.enter_context(tc.psum_pool(name="psum", bufs=1))
-        ctx.enter_context(tc.manual_schedule())
 
         ident = keep.tile([P, P], F32, name="ident")
         warm = keep.tile([P, 1], F32, name="warm")
@@ -196,13 +195,13 @@ def tile_gdn_t_kernel(tc, x, beta, gamma, out):
             c = k + 3 if k <= 0 else k + 4
             mx(k, 0)
             mx(k, 1)
-            rtr(k - 1, 0)
             xt(c, 0)
+            rtr(k - 1, 0)
             rtr(k - 1, 1)
-            ars(k, 0)
             for (pc, ph) in pending:
                 sq_scalar(pc, ph)
             pending = []
+            ars(k, 0)
             ars(k, 1)
             mul_store(k - 1, 0)
             mul_store(k - 1, 1)
@@ -225,8 +224,8 @@ def tile_gdn_t_kernel(tc, x, beta, gamma, out):
                 g_chain(1, 2)
             mx(k, 2)
             mx(k, 3)
-            rtr(k - 1, 2)
             xt(c, 1)
+            rtr(k - 1, 2)
             rtr(k - 1, 3)
             ars(k, 2)
             ars(k, 3)

from contextlib import ExitStack

import concourse.masks as masks
import concourse.mybir as mybir

F32 = mybir.dt.float32
BF16 = mybir.dt.bfloat16
U32 = mybir.dt.uint32
U8 = mybir.dt.uint8
FP8X4 = mybir.dt.float8_e4m3fn_x4
ACT = mybir.ActivationFunctionType
ALU = mybir.AluOpType

P = 128
N_ROWS = 10240
CH = 512
CHUNK = 512
NCH = N_ROWS // CHUNK
FLOPS = 2 * N_ROWS * CH * CH

PEDESTAL = 2.0 ** -36
BETA_BOUND = (1e-6 + PEDESTAL) ** 0.5

PL = 3
QL = 2
NM = 3
NR = 3
NSQ = 6
NCD = 4
NRT = 3
NO = 4
NTMP = 3


HEAD = 4


def head_engine(c, h):
    if h == 1 and c != 1:
        return "V"
    return "S"


def tile_gdn_t_kernel(tc, x, beta, gamma, out):
    nc = tc.nc
    with ExitStack() as ctx:
        keep = ctx.enter_context(tc.tile_pool(name="keep", bufs=1))
        psum = ctx.enter_context(tc.psum_pool(name="psum", bufs=1))

        ident = keep.tile([P, P], F32, name="ident")
        warm = keep.tile([P, 1], F32, name="warm")
        warm2 = keep.tile([P, 1], F32, name="warm2")
        gam = keep.tile([P, 4, CH], BF16, name="gam")
        bet = keep.tile([4, P], BF16, name="bet")
        bz = keep.tile([P, P], F32, name="bz")
        b1 = keep.tile([P, 4], F32, name="b1")
        b2 = keep.tile([P, 4], F32, name="b2")
        b_sb = keep.tile([P, 4], F32, name="b_sb")
        gw = [keep.tile([P, 1024], BF16, name="gw%d" % i) for i in range(2)]
        g2 = [keep.tile([P, 1024], F32, name="g2%d" % i) for i in range(2)]
        gq = keep.tile([P, 2048], BF16, name="gq", align_bytes=64)
        g_cd = keep.tile([P, CH], U32, name="g_cd", align_bytes=64)
        g_sc = keep.tile([P, CH], U8, name="g_sc", align_bytes=64)
        xs = [keep.tile([P, 4, CH], BF16, name="x%d" % c) for c in range(NCH)]
        sq = [keep.tile([P, 2048], BF16, name="sq%d" % i, align_bytes=64) for i in range(NSQ)]
        tmp = [keep.tile([P, 1024], BF16, name="tmp%d" % i) for i in range(NTMP)]
        cd = [keep.tile([P, CHUNK], U32, name="cd%d" % i, align_bytes=64) for i in range(NCD)]
        sc = [keep.tile([P, CHUNK], U8, name="sc%d" % i, align_bytes=64) for i in range(NCD)]
        rt = [keep.tile([P, 4, CHUNK], F32, name="rt%d" % i) for i in range(NRT)]
        ot = [keep.tile([P, 4, CH], F32, name="ot%d" % i) for i in range(NO)]

        xb = [psum.tile([P, 512], F32, name="xb%d" % i) for i in range(2)]
        mb = [psum.tile([P, 512], F32, name="mb%d" % i) for i in range(NM)]
        rb = [psum.tile([P, 512], F32, name="rb%d" % i) for i in range(NR)]

        xv = x.rearrange("(c p r) j -> c p r j", p=P, r=4)
        ov = out.rearrange("(c p r) i -> c p r i", p=P, r=4)
        gv = gamma.rearrange("(m p) j -> p m j", p=P)

        nc.scalar.dma_start(out=bet[:], in_=beta.rearrange("(m p) -> m p", p=P))
        nc.sync.dma_start(out=gam[:, 0:2, :], in_=gv[:, 0:2, :])
        nc.sync.dma_start(out=xs[0][:, 0:2, :], in_=xv[0, :, 0:2, :])
        nc.sync.dma_start(out=gam[:, 2:4, :], in_=gv[:, 2:4, :])
        nc.sync.dma_start(out=xs[0][:, 2:4, :], in_=xv[0, :, 2:4, :])
        for c in range(1, NCH):
            nc.sync.dma_start(out=xs[c][:], in_=xv[c, :, :, :])

        masks.make_identity(nc, ident[:])
        nc.vector.memset(warm[:], 1.0)
        nc.scalar.activation(out=warm2[:], in_=warm[:], func=ACT.Abs_reciprocal_sqrt)
        nc.vector.memset(bz[:], 0.0)
        nc.vector.tensor_copy(out=bz[0:4, :], in_=bet[:])
        nc.tensor.transpose(rb[0][:, 0:P], bz[:], ident[:])
        nc.vector.tensor_scalar_max(out=b1[:], in0=rb[0][:, 0:4], scalar1=BETA_BOUND)
        nc.vector.tensor_tensor(out=b2[:], in0=b1[:], in1=b1[:], op=ALU.mult)
        nc.vector.tensor_scalar_add(out=b_sb[:], in0=b2[:], scalar1=-PEDESTAL)

        def words_to_bank(bank, src, half):
            for u in range(2):
                col = u * 256 + half * P
                nc.tensor.transpose(bank[:, col:col + P], src.bitcast(F32)[:, u * P:(u + 1) * P], ident[:])

        def bank_words(bank):
            return bank[:].rearrange("p (u n) -> p n u", u=2)

        def grouped_words(dst):
            return dst.bitcast(F32).rearrange("p (n u) -> p n u", u=2)

        def g_turn(hb):
            for mm in range(2):
                words_to_bank(mb[hb], gam[:, 2 * hb + mm, :], mm)
            nc.scalar.copy(out=grouped_words(gw[hb][:]), in_=bank_words(mb[hb]))

        def g_chain(hb, step):
            cols = slice(hb * 1024, (hb + 1) * 1024)
            wcols = slice(hb * 256, (hb + 1) * 256)
            if step == 0:
                nc.vector.scalar_tensor_tensor(out=g2[hb][:], in0=gw[hb][:], scalar=0.0, in1=gw[hb][:],
                                               op0=ALU.max, op1=ALU.mult)
            elif step == 1:
                nc.vector.tensor_scalar(out=gq[:, cols], in0=g2[hb][:], scalar1=PEDESTAL, scalar2=-PEDESTAL,
                                        op0=ALU.max, op1=ALU.add)
            else:
                nc.vector.quantize_mx(out=g_cd[:, wcols].bitcast(FP8X4), scales=g_sc[:, wcols], in_=gq[:, cols])

        def ok(c):
            return 0 <= c < NCH

        def xt(c, h):
            if ok(c):
                for rr in range(2):
                    words_to_bank(xb[h], xs[c][:, 2 * h + rr, :], rr)

        def sq_dst(c, h):
            return sq[c % NSQ][:, h * 1024:(h + 1) * 1024]

        def sq_scalar(c, h):
            nc.scalar.activation(
                out=sq_dst(c, h).rearrange("p (n u e) -> p n u e", u=2, e=2),
                in_=xb[h][:].bitcast(BF16).rearrange("p (u n e) -> p n u e", u=2, e=2),
                func=ACT.Square)

        def sq_words(c, h):
            nc.vector.tensor_copy(out=grouped_words(tmp[(2 * c + h) % NTMP][:]), in_=bank_words(xb[h]))

        def sq_mul(c, h, eng):
            t = tmp[(2 * c + h) % NTMP]
            eng.tensor_tensor(out=sq_dst(c, h), in0=t[:], in1=t[:], op=ALU.mult)

        def quant(c):
            if ok(c):
                nc.vector.quantize_mx(out=cd[c % NCD][:].bitcast(FP8X4), scales=sc[c % NCD][:], in_=sq[c % NSQ][:])

        def mx(c, m):
            if ok(c):
                cols = slice(m * P, (m + 1) * P)
                nc.tensor.matmul_mx(out=mb[(4 * c + m) % NM][:],
                                    lhsT=g_cd[:, cols].bitcast(FP8X4), lhsT_scale=g_sc[:, cols],
                                    rhs=cd[c % NCD][:].bitcast(FP8X4), rhs_scale=sc[c % NCD][:],
                                    start=True, stop=True)

        def ars(c, m):
            if ok(c):
                nc.scalar.activation(out=rt[c % NRT][:, m, :], in_=mb[(4 * c + m) % NM][:],
                                     func=ACT.Abs_reciprocal_sqrt, bias=b_sb[:, m:m + 1], scale=1.0)

        def rtr(c, r):
            if ok(c):
                bank = rb[(4 * c + r) % NR]
                for m in range(4):
                    nc.tensor.transpose(bank[:, m * P:(m + 1) * P], rt[c % NRT][:, m, r * P:(r + 1) * P], ident[:])

        def mul(c, r):
            if ok(c):
                nc.vector.tensor_tensor(out=ot[c % NO][:, r, :], in0=rb[(4 * c + r) % NR][:], in1=xs[c][:, r, :],
                                        op=ALU.mult)

        def store(c, r0, r1):
            if ok(c):
                nc.sync.dma_start(out=ov[c, :, r0:r1, :], in_=ot[c % NO][:, r0:r1, :])

        def mul_store(c, r):
            mul(c, r)
            if c == NCH - 1:
                store(c, r, r + 1)
            elif r % 2 == 1:
                store(c, r - 1, r + 1)

        g_turn(0)
        g_chain(0, 0)
        g_chain(0, 1)
        g_chain(0, 2)
        pending = []
        for k in range(-PL, NCH + 1):
            c = k + 3 if k <= 0 else k + 4
            mx(k, 0)
            mx(k, 1)
            xt(c, 0)
            rtr(k - 1, 0)
            rtr(k - 1, 1)
            for (pc, ph) in pending:
                sq_scalar(pc, ph)
            pending = []
            ars(k, 0)
            ars(k, 1)
            mul_store(k - 1, 0)
            mul_store(k - 1, 1)
            if k == -PL + 1:
                g_chain(1, 0)
            e0 = "G" if c >= HEAD else head_engine(c, 0)
            if ok(c) and e0 == "S":
                sq_scalar(c, 0)
            if ok(c) and e0 != "S":
                sq_words(c, 0)
            if ok(c) and e0 == "V":
                sq_mul(c, 0, nc.vector)
            quant(k + QL)
            if ok(c) and e0 == "G":
                sq_mul(c, 0, nc.gpsimd)
            if k == -PL:
                g_turn(1)
            if k == -PL + 1:
                g_chain(1, 1)
                g_chain(1, 2)
            mx(k, 2)
            mx(k, 3)
            xt(c, 1)
            rtr(k - 1, 2)
            rtr(k - 1, 3)
            ars(k, 2)
            ars(k, 3)
            mul_store(k - 1, 2)
            mul_store(k - 1, 3)
            e1 = "S" if c >= HEAD else head_engine(c, 1)
            if ok(c) and e1 == "S":
                pending.append((c, 1))
            if ok(c) and e1 == "V":
                sq_words(c, 1)
                sq_mul(c, 1, nc.vector)
            if k == 0:
                xt(4, 0)
                sq_words(4, 0)
                sq_mul(4, 0, nc.gpsimd)
                xt(4, 1)
                pending.append((4, 1))
